import numpy as np
import ml_dtypes


def mxq(x, axis, fmt="e4m3"):
    dtype, down = {"e4m3": (ml_dtypes.float8_e4m3fn, 7), "e5m2": (ml_dtypes.float8_e5m2, 14)}[fmt]
    v = np.moveaxis(np.asarray(x, np.float32).astype(ml_dtypes.bfloat16).astype(np.float64), axis, -1)
    blocks = v.reshape(v.shape[:-1] + (-1, 32))
    amax = np.abs(blocks).max(-1, keepdims=True)
    byte = np.maximum(np.where(amax > 0, np.frexp(amax)[1] - 1 + 127, 0) - down, 1)
    scale = np.exp2(byte - 127.0)
    codes = (blocks / scale).astype(np.float32).astype(dtype).astype(np.float64)
    return np.moveaxis((codes * scale).reshape(v.shape), -1, axis)


WIDE = False


def mx_kscale(k):
    if not WIDE:
        return np.ones(k)
    levels = np.array([10, -10, 5, -5, 0])
    a = np.random.permutation(np.resize(levels, k // 512 * 4)).reshape(k // 512, 4)
    idx = np.arange(k)
    return np.exp2(a[idx // 512, idx % 128 // 32])


BF16 = ml_dtypes.bfloat16


def bf(x):
    return np.asarray(x, np.float32).astype(BF16)


def f64(x):
    return np.asarray(x).astype(np.float64)


E2M1 = np.array([0.0, 0.5, 1.0, 1.5, 2.0, 3.0, 4.0, 6.0, -0.0, -0.5, -1.0, -1.5, -2.0, -3.0, -4.0, -6.0])


def pack_weight(w, fmt):
    k, n = w.shape
    w = f64(bf(w)).reshape(k // 32, 32, n)
    amax = np.abs(w).max(1)
    if fmt == "e4m3":
        byte = np.frexp(amax)[1] - 1 + 127 - 7
    else:
        mant, ex = np.frexp(amax / 6.0)
        byte = np.where(mant > 0.5, ex, ex - 1) + 127
    byte = np.clip(np.where(amax > 0, byte, 1), 1, 254)
    scaled = (w * np.exp2(127.0 - byte)[:, None, :]).reshape(k, n).astype(np.float32)
    by_word = np.ascontiguousarray(scaled.reshape(k // 512, 128, 4, n).transpose(0, 1, 3, 2))
    if fmt == "e4m3":
        words = by_word.astype(ml_dtypes.float8_e4m3fn).view(np.uint8)
    else:
        c = by_word.astype(ml_dtypes.float4_e2m1fn).view(np.uint8) & 0xF
        words = c[..., 0::2] | (c[..., 1::2] << 4)
    return np.ascontiguousarray(words), np.ascontiguousarray(byte.astype(np.uint8).reshape(k // 512, 16, n))


def unpack_weight(words, scales, fmt):
    g, p, n, _ = words.shape
    if fmt == "e4m3":
        vals = np.ascontiguousarray(words).view(ml_dtypes.float8_e4m3fn).astype(np.float64)
    else:
        nib = np.empty((g, p, n, 4), np.uint8)
        nib[..., 0::2] = words & 0xF
        nib[..., 1::2] = words >> 4
        vals = E2M1[nib]
    vals = vals * np.repeat(np.exp2(scales.astype(np.float64) - 127.0), 8, axis=1)[..., None]
    return vals.transpose(0, 1, 3, 2).reshape(g * 512, n)


B, I, H = 128, 2048, 2048
EPS = 1e-5
FMT = "e4m3"


def sigmoid(v):
    return 1.0 / (1.0 + np.exp(-v))


def ln(v, g, b):
    m = v.mean(-1, keepdims=True)
    var = np.square(v - m).mean(-1, keepdims=True)
    return (v - m) / np.sqrt(var + EPS) * g + b


def setup_inputs():
    s, t = mx_kscale(I), mx_kscale(H)
    d = {"x": bf(np.random.standard_normal((B, I)) * s), "h": bf(np.random.standard_normal((B, H)) * t),
         "c": bf(np.random.standard_normal((B, H))), "ic_tilde": bf(0.35 * np.random.standard_normal((B, H)))}
    for g in ("f", "o"):
        w = np.random.standard_normal((H, I)) / np.sqrt(I) / s[None, :]
        words, scales = pack_weight(np.ascontiguousarray(w.T), FMT)
        d["W" + g + "_w_words"] = words
        d["W" + g + "_w_scales"] = scales
        d["W" + g + "_b"] = bf(np.random.standard_normal(H) * 0.5)
        u = np.random.standard_normal((H, H)) / np.sqrt(H) / t[None, :]
        words, scales = pack_weight(np.ascontiguousarray(u.T), FMT)
        d["U" + g + "_w_words"] = words
        d["U" + g + "_w_scales"] = scales
        d["ln" + g + "_g"] = bf(1.0 + 0.2 * np.random.standard_normal(H))
        d["ln" + g + "_b"] = bf(0.2 * np.random.standard_normal(H))
    return d


def reference(x, h, c, ic_tilde, Wf_w_words, Wf_w_scales, Wf_b, Uf_w_words, Uf_w_scales, lnf_g, lnf_b,
              Wo_w_words, Wo_w_scales, Wo_b, Uo_w_words, Uo_w_scales, lno_g, lno_b):
    xq = mxq(f64(x), 1, "e4m3")
    hq = mxq(f64(h), 1, "e4m3")
    pre_f = (xq @ unpack_weight(Wf_w_words, Wf_w_scales, FMT)) + f64(Wf_b) + (hq @ unpack_weight(Uf_w_words, Uf_w_scales, FMT))
    pre_o = (xq @ unpack_weight(Wo_w_words, Wo_w_scales, FMT)) + f64(Wo_b) + (hq @ unpack_weight(Uo_w_words, Uo_w_scales, FMT))
    f = sigmoid(ln(pre_f, f64(lnf_g), f64(lnf_b)))
    o = sigmoid(ln(pre_o, f64(lno_g), f64(lno_b)))
    c_new = f * f64(c) + f64(ic_tilde)
    h_new = o * np.tanh(c_new)
    return (h_new, c_new)

@@ -1,0 +1,277 @@
+from contextlib import ExitStack
+
+import concourse.mybir as mybir
+from concourse.masks import make_identity
+
+F32 = mybir.dt.float32
+BF16 = mybir.dt.bfloat16
+I32 = mybir.dt.int32
+U32 = mybir.dt.uint32
+U8 = mybir.dt.uint8
+FP8X4 = mybir.dt.float8_e4m3fn_x4
+ALU = mybir.AluOpType
+ACT = mybir.ActivationFunctionType
+AXIS = mybir.AxisListType
+
+P = 128
+PACK = 4
+K_PASS = P * PACK
+K = 2048
+GROUPS = K // K_PASS
+N = 2048
+N_TILE = 512
+N_TILES = N // N_TILE
+EPS = 1e-5
+
+FLOPS = 4 * 2 * P * K * N
+
+FORGET_ROUNDS = ((0, 1, 2, 3),)
+OUTPUT_ROUNDS = ((0, 1, 2), (3,))
+
+
+def tile_cols(j):
+    return slice(j * N_TILE, (j + 1) * N_TILE)
+
+
+def load_scale_planes(nc, planes, w, scales):
+    for quadrant in range(4):
+        nc.sync.dma_start(
+            out=planes[32 * quadrant : 32 * quadrant + 16, w, :].bitcast(I32),
+            in_=scales[:, 4 * quadrant : 4 * quadrant + 4, :].bitcast(I32),
+        )
+
+
+def load_weight_round(nc, words, dram_words, tiles):
+    cols = slice(tiles[0] * N_TILE, (tiles[-1] + 1) * N_TILE)
+    for g in range(GROUPS):
+        nc.sync.dma_start(
+            out=words[:, g, cols].bitcast(I32),
+            in_=dram_words[g, :, cols, :].rearrange("p n t -> p (n t)").bitcast(I32),
+        )
+
+
+def quantise_activation(nc, pool, psum, raw, ident, codes, scales, name):
+    raw_words = raw[:].bitcast(F32)
+    grouped = pool.tile([P, GROUPS, P, PACK], BF16, align_bytes=64, name=name)
+    grouped_words = grouped[:].bitcast(F32)
+    words_per_group = K_PASS // 2
+    for pair in range(GROUPS // 2):
+        flipped = psum.tile([P, 2, 2, P], F32, tag="bank")
+        for i in range(2):
+            g = 2 * pair + i
+            for u in range(2):
+                nc.tensor.transpose(
+                    flipped[:, i, u, :],
+                    raw_words[:, g * words_per_group + u : (g + 1) * words_per_group : 2],
+                    ident[:],
+                )
+        nc.vector.tensor_copy(
+            out=grouped_words[:, 2 * pair : 2 * pair + 2, :, :],
+            in_=flipped[:].rearrange("p g u m -> p g m u"),
+        )
+    nc.vector.quantize_mx(
+        out=codes[:].bitcast(FP8X4),
+        scales=scales[:],
+        in_=grouped[:].rearrange("p g m t -> p (g m t)"),
+    )
+
+
+def spread_row(nc, psum, rows, r, ident_bf, spread):
+    pick_row = ident_bf[:, r : r + 1].to_broadcast([P, P])
+    for half in range(2):
+        bank = psum.tile([P, 2 * N_TILE], BF16, tag="bank")
+        for i in range(2):
+            nc.tensor.matmul(
+                out=bank[:, tile_cols(i)],
+                lhsT=pick_row,
+                rhs=rows[:, tile_cols(2 * half + i)],
+                start=True,
+                stop=True,
+            )
+        nc.scalar.copy(out=spread[:, half * 2 * N_TILE : (half + 1) * 2 * N_TILE], in_=bank[:])
+
+
+def gate_round(nc, psum, tiles, operands, planes, bias, pre, sums):
+    acc = {}
+    for j in tiles:
+        acc[j] = psum.tile([P, N_TILE], F32, tag="bank", name="acc%d" % j)
+    passes = len(operands) * GROUPS
+    for i, (codes, scales, words, w) in enumerate(operands):
+        for g in range(GROUPS):
+            batch_cols = slice(g * P, (g + 1) * P)
+            for j in tiles:
+                nc.tensor.matmul_mx(
+                    out=acc[j][:],
+                    lhsT=codes[:, batch_cols].bitcast(FP8X4),
+                    lhsT_scale=scales[:, batch_cols],
+                    rhs=words[:, g, tile_cols(j)].bitcast(FP8X4),
+                    rhs_scale=planes[PACK * g : P, w, tile_cols(j)],
+                    start=(i * GROUPS + g == 0),
+                    stop=(i * GROUPS + g == passes - 1),
+                )
+    for j in tiles:
+        nc.vector.scalar_tensor_tensor(
+            out=pre[:, tile_cols(j)],
+            in0=acc[j][:],
+            scalar=1.0,
+            in1=bias[:, tile_cols(j)],
+            op0=ALU.mult,
+            op1=ALU.add,
+            accum_out=sums[:, j : j + 1],
+        )
+
+
+def row_statistics(nc, work, small, pre, sums, neg_half):
+    total = small.tile([P, 1], F32)
+    nc.vector.tensor_reduce(out=total[:], in_=sums[:], axis=AXIS.X, op=ALU.add)
+    neg_mean = small.tile([P, 1], F32)
+    nc.vector.tensor_scalar_mul(out=neg_mean[:], in0=total[:], scalar1=-1.0 / N)
+
+    squares = work.tile([P, N], BF16)
+    dev_sq = small.tile([P, 1], F32)
+    nc.scalar.activation(
+        out=squares[:], in_=pre[:], func=ACT.Square, bias=neg_mean[:], scale=1.0, accum_out=dev_sq[:]
+    )
+    var_eps = small.tile([P, 1], F32)
+    nc.gpsimd.tensor_scalar(
+        out=var_eps[:], in0=dev_sq[:], scalar1=1.0 / N, scalar2=EPS, op0=ALU.mult, op1=ALU.add
+    )
+    rstd = small.tile([P, 1], F32)
+    nc.gpsimd.tensor_tensor(out=rstd[:], in0=var_eps[:], in1=neg_half[:], op=ALU.pow)
+    return neg_mean, rstd
+
+
+def centre(nc, pre, neg_mean, gain, gate):
+    for j in range(N_TILES):
+        nc.vector.scalar_tensor_tensor(
+            out=gate[:, tile_cols(j)],
+            in0=pre[:, tile_cols(j)],
+            scalar=neg_mean[:],
+            in1=gain[:, tile_cols(j)],
+            op0=ALU.add,
+            op1=ALU.mult,
+        )
+
+
+def squash(nc, gate, cols, rstd, shift):
+    nc.vector.scalar_tensor_tensor(
+        out=gate[:, cols], in0=gate[:, cols], scalar=rstd[:], in1=shift[:, cols], op0=ALU.mult, op1=ALU.add
+    )
+    nc.scalar.activation(out=gate[:, cols], in_=gate[:, cols], func=ACT.Sigmoid)
+
+
+def tile_layernormlstmcell_pb_kernel(
+    tc,
+    x,
+    h,
+    c,
+    ic_tilde,
+    Wf_w_words,
+    Wf_w_scales,
+    Wf_b,
+    Uf_w_words,
+    Uf_w_scales,
+    lnf_g,
+    lnf_b,
+    Wo_w_words,
+    Wo_w_scales,
+    Wo_b,
+    Uo_w_words,
+    Uo_w_scales,
+    lno_g,
+    lno_b,
+    out_0,
+    out_1,
+):
+    nc = tc.nc
+    h_new, c_new = out_0, out_1
+    with ExitStack() as stack:
+        keep = stack.enter_context(tc.tile_pool(name="keep", bufs=1))
+        small = stack.enter_context(tc.tile_pool(name="small", bufs=2))
+        psum = stack.enter_context(tc.psum_pool(name="psum", bufs=8))
+
+        planes = keep.tile([P, 4, N], U8, align_bytes=64)
+        words = []
+        for w in range(4):
+            words.append(keep.tile([P, GROUPS, N], U32, align_bytes=64, name="words%d" % w))
+        x_codes = keep.tile([P, GROUPS * P], U32, align_bytes=64)
+        x_scales = keep.tile([P, GROUPS * P], U8, align_bytes=64)
+        h_codes = keep.tile([P, GROUPS * P], U32, align_bytes=64)
+        h_scales = keep.tile([P, GROUPS * P], U8, align_bytes=64)
+        c_old = keep.tile([P, N], BF16)
+        ic_sb = keep.tile([P, N], BF16)
+        neg_half = keep.tile([P, 1], F32)
+        vectors = (Wf_b, lnf_g, lnf_b, Wo_b, lno_g, lno_b)
+        spread = []
+        for r in range(len(vectors)):
+            spread.append(keep.tile([P, N], BF16, name="spread%d" % r))
+        bias_f, gain_f, shift_f, bias_o, gain_o, shift_o = spread
+
+        with tc.tile_pool(name="head", bufs=1) as head:
+            rows = head.tile([P, N], BF16)
+            nc.vector.memset(rows[:], 0.0)
+            nc.vector.memset(planes[:].rearrange("p w n -> p (w n)").bitcast(I32), 0)
+            nc.vector.memset(neg_half[:], -0.5)
+            ident = head.tile([P, P], F32)
+            make_identity(nc, ident[:])
+            ident_bf = head.tile([P, P], BF16)
+            make_identity(nc, ident_bf[:])
+
+            for r, vector in enumerate(vectors):
+                nc.scalar.dma_start(out=rows[r : r + 1, :], in_=vector.unsqueeze(0))
+            x_raw = head.tile([P, K], BF16)
+            nc.sync.dma_start(out=x_raw[:], in_=x)
+            h_raw = head.tile([P, K], BF16)
+            nc.sync.dma_start(out=h_raw[:], in_=h)
+            for w, dram_scales in enumerate((Wf_w_scales, Uf_w_scales, Wo_w_scales, Uo_w_scales)):
+                load_scale_planes(nc, planes, w, dram_scales)
+            for tiles in FORGET_ROUNDS:
+                load_weight_round(nc, words[0], Wf_w_words, tiles)
+                load_weight_round(nc, words[1], Uf_w_words, tiles)
+            nc.sync.dma_start(out=c_old[:], in_=c)
+            nc.sync.dma_start(out=ic_sb[:], in_=ic_tilde)
+            for tiles in OUTPUT_ROUNDS:
+                load_weight_round(nc, words[2], Wo_w_words, tiles)
+                load_weight_round(nc, words[3], Uo_w_words, tiles)
+
+            quantise_activation(nc, head, psum, x_raw, ident, x_codes, x_scales, "x_grouped")
+            quantise_activation(nc, head, psum, h_raw, ident, h_codes, h_scales, "h_grouped")
+            for r in range(len(vectors)):
+                spread_row(nc, psum, rows, r, ident_bf, spread[r])
+
+        work = stack.enter_context(tc.tile_pool(name="work", bufs=1))
+
+        pre_f = work.tile([P, N], F32, tag="pre")
+        sums_f = small.tile([P, N_TILES], F32)
+        operands_f = ((x_codes, x_scales, words[0], 0), (h_codes, h_scales, words[1], 1))
+        for tiles in FORGET_ROUNDS:
+            gate_round(nc, psum, tiles, operands_f, planes, bias_f, pre_f, sums_f)
+        neg_mean_f, rstd_f = row_statistics(nc, work, small, pre_f, sums_f, neg_half)
+        cell = work.tile([P, N], F32)
+        centre(nc, pre_f, neg_mean_f, gain_f, cell)
+        tanh_c = work.tile([P, N], F32)
+        for j in range(N_TILES + 1):
+            if j < N_TILES:
+                squash(nc, cell, tile_cols(j), rstd_f, shift_f)
+            if j > 0:
+                cols = tile_cols(j - 1)
+                nc.vector.tensor_tensor(out=cell[:, cols], in0=cell[:, cols], in1=c_old[:, cols], op=ALU.mult)
+                nc.vector.tensor_tensor(out=cell[:, cols], in0=cell[:, cols], in1=ic_sb[:, cols], op=ALU.add)
+                nc.scalar.activation(out=tanh_c[:, cols], in_=cell[:, cols], func=ACT.Tanh)
+        nc.sync.dma_start(out=c_new, in_=cell[:])
+
+        pre_o = work.tile([P, N], F32, tag="pre")
+        sums_o = small.tile([P, N_TILES], F32)
+        operands_o = ((x_codes, x_scales, words[2], 2), (h_codes, h_scales, words[3], 3))
+        for tiles in OUTPUT_ROUNDS:
+            gate_round(nc, psum, tiles, operands_o, planes, bias_o, pre_o, sums_o)
+        neg_mean_o, rstd_o = row_statistics(nc, work, small, pre_o, sums_o, neg_half)
+        hidden = work.tile([P, N], F32)
+        centre(nc, pre_o, neg_mean_o, gain_o, hidden)
+        for j in range(N_TILES + 1):
+            if j < N_TILES:
+                squash(nc, hidden, tile_cols(j), rstd_o, shift_o)
+            if j > 0:
+                cols = tile_cols(j - 1)
+                nc.vector.tensor_tensor(out=hidden[:, cols], in0=hidden[:, cols], in1=tanh_c[:, cols], op=ALU.mult)
+                nc.sync.dma_start(out=h_new[:, cols], in_=hidden[:, cols])

@@ -76,8 +76,9 @@ def quantise_activation(nc, pool, psum, raw, ident, codes, scales, name):
     )
 
 
-def spread_row(nc, psum, rows, r, ident_bf, spread):
+def spread_row(nc, psum, rows, r, ident_bf):
     pick_row = ident_bf[:, r : r + 1].to_broadcast([P, P])
+    banks = []
     for half in range(2):
         bank = psum.tile([P, 2 * N_TILE], BF16, tag="bank")
         for i in range(2):
@@ -88,10 +89,24 @@ def spread_row(nc, psum, rows, r, ident_bf, spread):
                 start=True,
                 stop=True,
             )
-        nc.scalar.copy(out=spread[:, half * 2 * N_TILE : (half + 1) * 2 * N_TILE], in_=bank[:])
+        banks.append(bank)
+    return banks
 
 
-def gate_round(nc, psum, tiles, operands, planes, bias, pre, sums):
+def spread_row_in_psum(nc, psum, rows, r, ident_bf):
+    banks = spread_row(nc, psum, rows, r, ident_bf)
+    return [banks[j // 2][:, tile_cols(j % 2)] for j in range(N_TILES)]
+
+
+def spread_row_in_sbuf(nc, psum, keep, rows, r, ident_bf):
+    banks = spread_row(nc, psum, rows, r, ident_bf)
+    spread = keep.tile([P, N], BF16, name="spread%d" % r)
+    for half in range(2):
+        nc.scalar.copy(out=spread[:, half * 2 * N_TILE : (half + 1) * 2 * N_TILE], in_=banks[half][:])
+    return [spread[:, tile_cols(j)] for j in range(N_TILES)]
+
+
+def gate_round(nc, psum, tiles, operands, planes, bias, pre, stats):
     acc = {}
     for j in tiles:
         acc[j] = psum.tile([P, N_TILE], F32, tag="bank", name="acc%d" % j)
@@ -110,54 +125,33 @@ def gate_round(nc, psum, tiles, operands, planes, bias, pre, sums):
                     stop=(i * GROUPS + g == passes - 1),
                 )
     for j in tiles:
-        nc.vector.scalar_tensor_tensor(
-            out=pre[:, tile_cols(j)],
-            in0=acc[j][:],
-            scalar=1.0,
-            in1=bias[:, tile_cols(j)],
-            op0=ALU.mult,
-            op1=ALU.add,
-            accum_out=sums[:, j : j + 1],
-        )
+        nc.vector.tensor_tensor(out=pre[:, tile_cols(j)], in0=acc[j][:], in1=bias[j], op=ALU.add)
+        nc.vector.bn_stats(out=stats[:, j, :], in_=pre[:, tile_cols(j)])
 
 
-def row_statistics(nc, work, small, pre, sums, neg_half):
-    total = small.tile([P, 1], F32)
-    nc.vector.tensor_reduce(out=total[:], in_=sums[:], axis=AXIS.X, op=ALU.add)
-    neg_mean = small.tile([P, 1], F32)
-    nc.vector.tensor_scalar_mul(out=neg_mean[:], in0=total[:], scalar1=-1.0 / N)
-
-    squares = work.tile([P, N], BF16)
-    dev_sq = small.tile([P, 1], F32)
-    nc.scalar.activation(
-        out=squares[:], in_=pre[:], func=ACT.Square, bias=neg_mean[:], scale=1.0, accum_out=dev_sq[:]
-    )
+def layer_norm_sigmoid(nc, small, pre, stats, gain, shift, neg_half, gate, finish):
+    mean_var = small.tile([P, 2], F32)
+    nc.vector.bn_aggr(out=mean_var[:], in_=stats[:].rearrange("p j s -> p (j s)"))
     var_eps = small.tile([P, 1], F32)
-    nc.gpsimd.tensor_scalar(
-        out=var_eps[:], in0=dev_sq[:], scalar1=1.0 / N, scalar2=EPS, op0=ALU.mult, op1=ALU.add
-    )
+    nc.vector.tensor_scalar_add(out=var_eps[:], in0=mean_var[:, 1:2], scalar1=EPS)
     rstd = small.tile([P, 1], F32)
     nc.gpsimd.tensor_tensor(out=rstd[:], in0=var_eps[:], in1=neg_half[:], op=ALU.pow)
-    return neg_mean, rstd
-
-
-def centre(nc, pre, neg_mean, gain, gate):
-    for j in range(N_TILES):
-        nc.vector.scalar_tensor_tensor(
-            out=gate[:, tile_cols(j)],
-            in0=pre[:, tile_cols(j)],
-            scalar=neg_mean[:],
-            in1=gain[:, tile_cols(j)],
-            op0=ALU.add,
-            op1=ALU.mult,
-        )
-
-
-def squash(nc, gate, cols, rstd, shift):
-    nc.vector.scalar_tensor_tensor(
-        out=gate[:, cols], in0=gate[:, cols], scalar=rstd[:], in1=shift[:, cols], op0=ALU.mult, op1=ALU.add
-    )
-    nc.scalar.activation(out=gate[:, cols], in_=gate[:, cols], func=ACT.Sigmoid)
+    for step in range(N_TILES + 2):
+        if step < N_TILES:
+            cols = tile_cols(step)
+            nc.vector.scalar_tensor_tensor(
+                out=gate[:, cols], in0=pre[:, cols], scalar=mean_var[:, 0:1], in1=gain[step],
+                op0=ALU.subtract, op1=ALU.mult,
+            )
+        if 1 <= step <= N_TILES:
+            cols = tile_cols(step - 1)
+            nc.vector.scalar_tensor_tensor(
+                out=gate[:, cols], in0=gate[:, cols], scalar=rstd[:], in1=shift[step - 1],
+                op0=ALU.mult, op1=ALU.add,
+            )
+            nc.scalar.activation(out=gate[:, cols], in_=gate[:, cols], func=ACT.Sigmoid)
+        if step >= 2:
+            finish(step - 2)
 
 
 def tile_layernormlstmcell_pb_kernel(
@@ -201,20 +195,16 @@ def tile_layernormlstmcell_pb_kernel(
         c_old = keep.tile([P, N], BF16)
         ic_sb = keep.tile([P, N], BF16)
         neg_half = keep.tile([P, 1], F32)
+        rows = keep.tile([P, N], BF16)
+        ident_bf = keep.tile([P, P], BF16)
         vectors = (Wf_b, lnf_g, lnf_b, Wo_b, lno_g, lno_b)
-        spread = []
-        for r in range(len(vectors)):
-            spread.append(keep.tile([P, N], BF16, name="spread%d" % r))
-        bias_f, gain_f, shift_f, bias_o, gain_o, shift_o = spread
 
         with tc.tile_pool(name="head", bufs=1) as head:
-            rows = head.tile([P, N], BF16)
             nc.vector.memset(rows[:], 0.0)
             nc.vector.memset(planes[:].rearrange("p w n -> p (w n)").bitcast(I32), 0)
             nc.vector.memset(neg_half[:], -0.5)
             ident = head.tile([P, P], F32)
             make_identity(nc, ident[:])
-            ident_bf = head.tile([P, P], BF16)
             make_identity(nc, ident_bf[:])
 
             for r, vector in enumerate(vectors):
@@ -236,42 +226,44 @@ def tile_layernormlstmcell_pb_kernel(
 
             quantise_activation(nc, head, psum, x_raw, ident, x_codes, x_scales, "x_grouped")
             quantise_activation(nc, head, psum, h_raw, ident, h_codes, h_scales, "h_grouped")
-            for r in range(len(vectors)):
-                spread_row(nc, psum, rows, r, ident_bf, spread[r])
+
+        bias_f = spread_row_in_sbuf(nc, psum, keep, rows, 0, ident_bf)
+        gain_f = spread_row_in_sbuf(nc, psum, keep, rows, 1, ident_bf)
+        shift_f = spread_row_in_sbuf(nc, psum, keep, rows, 2, ident_bf)
+        bias_o = spread_row_in_sbuf(nc, psum, keep, rows, 3, ident_bf)
 
         work = stack.enter_context(tc.tile_pool(name="work", bufs=1))
 
         pre_f = work.tile([P, N], F32, tag="pre")
-        sums_f = small.tile([P, N_TILES], F32)
+        stats_f = small.tile([P, N_TILES, 6], F32)
         operands_f = ((x_codes, x_scales, words[0], 0), (h_codes, h_scales, words[1], 1))
         for tiles in FORGET_ROUNDS:
-            gate_round(nc, psum, tiles, operands_f, planes, bias_f, pre_f, sums_f)
-        neg_mean_f, rstd_f = row_statistics(nc, work, small, pre_f, sums_f, neg_half)
+            gate_round(nc, psum, tiles, operands_f, planes, bias_f, pre_f, stats_f)
         cell = work.tile([P, N], F32)
-        centre(nc, pre_f, neg_mean_f, gain_f, cell)
         tanh_c = work.tile([P, N], F32)
-        for j in range(N_TILES + 1):
-            if j < N_TILES:
-                squash(nc, cell, tile_cols(j), rstd_f, shift_f)
-            if j > 0:
-                cols = tile_cols(j - 1)
-                nc.vector.tensor_tensor(out=cell[:, cols], in0=cell[:, cols], in1=c_old[:, cols], op=ALU.mult)
-                nc.vector.tensor_tensor(out=cell[:, cols], in0=cell[:, cols], in1=ic_sb[:, cols], op=ALU.add)
-                nc.scalar.activation(out=tanh_c[:, cols], in_=cell[:, cols], func=ACT.Tanh)
+
+        def update_cell(j):
+            cols = tile_cols(j)
+            nc.vector.tensor_tensor(out=cell[:, cols], in0=cell[:, cols], in1=c_old[:, cols], op=ALU.mult)
+            nc.vector.tensor_tensor(out=cell[:, cols], in0=cell[:, cols], in1=ic_sb[:, cols], op=ALU.add)
+            nc.scalar.activation(out=tanh_c[:, cols], in_=cell[:, cols], func=ACT.Tanh)
+
+        layer_norm_sigmoid(nc, small, pre_f, stats_f, gain_f, shift_f, neg_half, cell, update_cell)
         nc.sync.dma_start(out=c_new, in_=cell[:])
 
+        gain_o = spread_row_in_psum(nc, psum, rows, 4, ident_bf)
+        shift_o = spread_row_in_psum(nc, psum, rows, 5, ident_bf)
         pre_o = work.tile([P, N], F32, tag="pre")
-        sums_o = small.tile([P, N_TILES], F32)
+        stats_o = small.tile([P, N_TILES, 6], F32)
         operands_o = ((x_codes, x_scales, words[2], 2), (h_codes, h_scales, words[3], 3))
         for tiles in OUTPUT_ROUNDS:
-            gate_round(nc, psum, tiles, operands_o, planes, bias_o, pre_o, sums_o)
-        neg_mean_o, rstd_o = row_statistics(nc, work, small, pre_o, sums_o, neg_half)
+            gate_round(nc, psum, tiles, operands_o, planes, bias_o, pre_o, stats_o)
         hidden = work.tile([P, N], F32)
-        centre(nc, pre_o, neg_mean_o, gain_o, hidden)
-        for j in range(N_TILES + 1):
-            if j < N_TILES:
-                squash(nc, hidden, tile_cols(j), rstd_o, shift_o)
-            if j > 0:
-                cols = tile_cols(j - 1)
-                nc.vector.tensor_tensor(out=hidden[:, cols], in0=hidden[:, cols], in1=tanh_c[:, cols], op=ALU.mult)
-                nc.sync.dma_start(out=h_new[:, cols], in_=hidden[:, cols])
+
+        def update_hidden(j):
+            cols = tile_cols(j)
+            engine = nc.gpsimd if j < N_TILES // 2 else nc.vector
+            engine.tensor_tensor(out=hidden[:, cols], in0=hidden[:, cols], in1=tanh_c[:, cols], op=ALU.mult)
+            nc.sync.dma_start(out=h_new[:, cols], in_=hidden[:, cols])
+
+        layer_norm_sigmoid(nc, small, pre_o, stats_o, gain_o, shift_o, neg_half, hidden, update_hidden)

@@ -35,9 +35,9 @@ def tile_cols(j):
 
 def load_scale_planes(nc, planes, w, scales):
     for quadrant in range(4):
-        nc.sync.dma_start(
-            out=planes[32 * quadrant : 32 * quadrant + 16, w, :].bitcast(I32),
-            in_=scales[:, 4 * quadrant : 4 * quadrant + 4, :].bitcast(I32),
+        nc.gpsimd.dma_start(
+            out=planes[32 * quadrant : 32 * quadrant + 16, w, :].bitcast(F32),
+            in_=scales[:, 4 * quadrant : 4 * quadrant + 4, :].bitcast(F32),
         )
 
 

@@ -25,7 +25,7 @@ EPS = 1e-5
 
 FLOPS = 4 * 2 * P * K * N
 
-FORGET_ROUNDS = ((0, 1, 2, 3),)
+FORGET_TILES = (0, 1, 2, 3)
 OUTPUT_ROUNDS = ((0, 1, 2), (3,))
 
 
@@ -106,25 +106,31 @@ def spread_row_in_sbuf(nc, psum, keep, rows, r, ident_bf):
     return [spread[:, tile_cols(j)] for j in range(N_TILES)]
 
 
-def gate_round(nc, psum, tiles, operands, planes, bias, pre, stats):
+def open_round(psum, tiles):
     acc = {}
     for j in tiles:
         acc[j] = psum.tile([P, N_TILE], F32, tag="bank", name="acc%d" % j)
-    passes = len(operands) * GROUPS
-    for i, (codes, scales, words, w) in enumerate(operands):
-        for g in range(GROUPS):
-            batch_cols = slice(g * P, (g + 1) * P)
-            for j in tiles:
-                nc.tensor.matmul_mx(
-                    out=acc[j][:],
-                    lhsT=codes[:, batch_cols].bitcast(FP8X4),
-                    lhsT_scale=scales[:, batch_cols],
-                    rhs=words[:, g, tile_cols(j)].bitcast(FP8X4),
-                    rhs_scale=planes[PACK * g : P, w, tile_cols(j)],
-                    start=(i * GROUPS + g == 0),
-                    stop=(i * GROUPS + g == passes - 1),
-                )
-    for j in tiles:
+    return acc
+
+
+def accumulate(nc, acc, operand, planes, first, last):
+    codes, scales, words, w = operand
+    for g in range(GROUPS):
+        batch_cols = slice(g * P, (g + 1) * P)
+        for j in acc:
+            nc.tensor.matmul_mx(
+                out=acc[j][:],
+                lhsT=codes[:, batch_cols].bitcast(FP8X4),
+                lhsT_scale=scales[:, batch_cols],
+                rhs=words[:, g, tile_cols(j)].bitcast(FP8X4),
+                rhs_scale=planes[PACK * g : P, w, tile_cols(j)],
+                start=(first and g == 0),
+                stop=(last and g == GROUPS - 1),
+            )
+
+
+def close_round(nc, acc, bias, pre, stats):
+    for j in acc:
         nc.vector.tensor_tensor(out=pre[:, tile_cols(j)], in0=acc[j][:], in1=bias[j], op=ALU.add)
         nc.vector.bn_stats(out=stats[:, j, :], in_=pre[:, tile_cols(j)])
 
@@ -200,24 +206,28 @@ def tile_layernormlstmcell_pb_kernel(
         vectors = (Wf_b, lnf_g, lnf_b, Wo_b, lno_g, lno_b)
 
         with tc.tile_pool(name="head", bufs=1) as head:
-            nc.vector.memset(rows[:], 0.0)
-            nc.vector.memset(planes[:].rearrange("p w n -> p (w n)").bitcast(I32), 0)
-            nc.vector.memset(neg_half[:], -0.5)
             ident = head.tile([P, P], F32)
             make_identity(nc, ident[:])
-            make_identity(nc, ident_bf[:])
+            for w in range(2):
+                nc.vector.memset(planes[:, w, :].bitcast(I32), 0)
+            nc.vector.memset(rows[:].bitcast(I32), 0)
+            for w in range(2, 4):
+                nc.vector.memset(planes[:, w, :].bitcast(I32), 0)
+            nc.vector.memset(neg_half[:], -0.5)
+            nc.vector.tensor_copy(out=ident_bf[:], in_=ident[:])
 
-            for r, vector in enumerate(vectors):
-                nc.scalar.dma_start(out=rows[r : r + 1, :], in_=vector.unsqueeze(0))
             x_raw = head.tile([P, K], BF16)
             nc.sync.dma_start(out=x_raw[:], in_=x)
             h_raw = head.tile([P, K], BF16)
             nc.sync.dma_start(out=h_raw[:], in_=h)
-            for w, dram_scales in enumerate((Wf_w_scales, Uf_w_scales, Wo_w_scales, Uo_w_scales)):
-                load_scale_planes(nc, planes, w, dram_scales)
-            for tiles in FORGET_ROUNDS:
-                load_weight_round(nc, words[0], Wf_w_words, tiles)
-                load_weight_round(nc, words[1], Uf_w_words, tiles)
+            load_scale_planes(nc, planes, 0, Wf_w_scales)
+            for r, vector in enumerate(vectors):
+                nc.gpsimd.dma_start(out=rows[r : r + 1, :], in_=vector.unsqueeze(0))
+            load_scale_planes(nc, planes, 1, Uf_w_scales)
+            load_scale_planes(nc, planes, 2, Wo_w_scales)
+            load_scale_planes(nc, planes, 3, Uo_w_scales)
+            load_weight_round(nc, words[0], Wf_w_words, FORGET_TILES)
+            load_weight_round(nc, words[1], Uf_w_words, FORGET_TILES)
             nc.sync.dma_start(out=c_old[:], in_=c)
             nc.sync.dma_start(out=ic_sb[:], in_=ic_tilde)
             for tiles in OUTPUT_ROUNDS:
@@ -227,18 +237,18 @@ def tile_layernormlstmcell_pb_kernel(
             quantise_activation(nc, head, psum, x_raw, ident, x_codes, x_scales, "x_grouped")
             quantise_activation(nc, head, psum, h_raw, ident, h_codes, h_scales, "h_grouped")
 
-        bias_f = spread_row_in_sbuf(nc, psum, keep, rows, 0, ident_bf)
-        gain_f = spread_row_in_sbuf(nc, psum, keep, rows, 1, ident_bf)
-        shift_f = spread_row_in_sbuf(nc, psum, keep, rows, 2, ident_bf)
-        bias_o = spread_row_in_sbuf(nc, psum, keep, rows, 3, ident_bf)
-
         work = stack.enter_context(tc.tile_pool(name="work", bufs=1))
 
         pre_f = work.tile([P, N], F32, tag="pre")
         stats_f = small.tile([P, N_TILES, 6], F32)
-        operands_f = ((x_codes, x_scales, words[0], 0), (h_codes, h_scales, words[1], 1))
-        for tiles in FORGET_ROUNDS:
-            gate_round(nc, psum, tiles, operands_f, planes, bias_f, pre_f, stats_f)
+        acc_f = open_round(psum, FORGET_TILES)
+        accumulate(nc, acc_f, (x_codes, x_scales, words[0], 0), planes, first=True, last=False)
+        bias_f = spread_row_in_sbuf(nc, psum, keep, rows, 0, ident_bf)
+        gain_f = spread_row_in_sbuf(nc, psum, keep, rows, 1, ident_bf)
+        shift_f = spread_row_in_sbuf(nc, psum, keep, rows, 2, ident_bf)
+        bias_o = spread_row_in_sbuf(nc, psum, keep, rows, 3, ident_bf)
+        accumulate(nc, acc_f, (h_codes, h_scales, words[1], 1), planes, first=False, last=True)
+        close_round(nc, acc_f, bias_f, pre_f, stats_f)
         cell = work.tile([P, N], F32)
         tanh_c = work.tile([P, N], F32)
 
@@ -255,9 +265,11 @@ def tile_layernormlstmcell_pb_kernel(
         shift_o = spread_row_in_psum(nc, psum, rows, 5, ident_bf)
         pre_o = work.tile([P, N], F32, tag="pre")
         stats_o = small.tile([P, N_TILES, 6], F32)
-        operands_o = ((x_codes, x_scales, words[2], 2), (h_codes, h_scales, words[3], 3))
         for tiles in OUTPUT_ROUNDS:
-            gate_round(nc, psum, tiles, operands_o, planes, bias_o, pre_o, stats_o)
+            acc_o = open_round(psum, tiles)
+            accumulate(nc, acc_o, (x_codes, x_scales, words[2], 2), planes, first=True, last=False)
+            accumulate(nc, acc_o, (h_codes, h_scales, words[3], 3), planes, first=False, last=True)
+            close_round(nc, acc_o, bias_o, pre_o, stats_o)
         hidden = work.tile([P, N], F32)
 
         def update_hidden(j):

@@ -26,11 +26,23 @@ EPS = 1e-5
 FLOPS = 4 * 2 * P * K * N
 
 FORGET_TILES = (0, 1, 2, 3)
+
+FORGET_WIDTHS = (512, 512, 512, 512)
+OUTPUT_WIDTHS = (512, 512, 512, 256, 256)
 OUTPUT_ROUNDS = ((0, 1, 2), (3,))
 
 
 def tile_cols(j):
     return slice(j * N_TILE, (j + 1) * N_TILE)
+
+
+def column_pieces(widths):
+    pieces = []
+    start = 0
+    for width in widths:
+        pieces.append(slice(start, start + width))
+        start += width
+    return pieces
 
 
 def load_scale_planes(nc, planes, w, scales):
@@ -95,7 +107,8 @@ def spread_row(nc, psum, rows, r, ident_bf):
 
 def spread_row_in_psum(nc, psum, rows, r, ident_bf):
     banks = spread_row(nc, psum, rows, r, ident_bf)
-    return [banks[j // 2][:, tile_cols(j % 2)] for j in range(N_TILES)]
+    width = 2 * N_TILE
+    return lambda cols: banks[cols.start // width][:, cols.start % width : (cols.stop - 1) % width + 1]
 
 
 def spread_row_in_sbuf(nc, psum, keep, rows, r, ident_bf):
@@ -103,7 +116,7 @@ def spread_row_in_sbuf(nc, psum, keep, rows, r, ident_bf):
     spread = keep.tile([P, N], BF16, name="spread%d" % r)
     for half in range(2):
         nc.scalar.copy(out=spread[:, half * 2 * N_TILE : (half + 1) * 2 * N_TILE], in_=banks[half][:])
-    return [spread[:, tile_cols(j)] for j in range(N_TILES)]
+    return lambda cols: spread[:, cols]
 
 
 def open_round(psum, tiles):
@@ -131,33 +144,33 @@ def accumulate(nc, acc, operand, planes, first, last):
 
 def close_round(nc, acc, bias, pre, stats):
     for j in acc:
-        nc.vector.tensor_tensor(out=pre[:, tile_cols(j)], in0=acc[j][:], in1=bias[j], op=ALU.add)
+        nc.vector.tensor_tensor(out=pre[:, tile_cols(j)], in0=acc[j][:], in1=bias(tile_cols(j)), op=ALU.add)
         nc.vector.bn_stats(out=stats[:, j, :], in_=pre[:, tile_cols(j)])
+        if j == 0:
+            nc.vector.tensor_scalar_add(out=stats[:, j, 2:3], in0=stats[:, j, 2:3], scalar1=N * EPS)
 
 
-def layer_norm_sigmoid(nc, small, pre, stats, gain, shift, neg_half, gate, finish):
+def layer_norm_sigmoid(nc, small, pre, stats, gain, shift, neg_half, gate, pieces, finish):
     mean_var = small.tile([P, 2], F32)
     nc.vector.bn_aggr(out=mean_var[:], in_=stats[:].rearrange("p j s -> p (j s)"))
-    var_eps = small.tile([P, 1], F32)
-    nc.vector.tensor_scalar_add(out=var_eps[:], in0=mean_var[:, 1:2], scalar1=EPS)
     rstd = small.tile([P, 1], F32)
-    nc.gpsimd.tensor_tensor(out=rstd[:], in0=var_eps[:], in1=neg_half[:], op=ALU.pow)
-    for step in range(N_TILES + 2):
-        if step < N_TILES:
-            cols = tile_cols(step)
+    nc.gpsimd.tensor_tensor(out=rstd[:], in0=mean_var[:, 1:2], in1=neg_half[:], op=ALU.pow)
+    for step in range(len(pieces) + 2):
+        if step < len(pieces):
+            cols = pieces[step]
             nc.vector.scalar_tensor_tensor(
-                out=gate[:, cols], in0=pre[:, cols], scalar=mean_var[:, 0:1], in1=gain[step],
+                out=gate[:, cols], in0=pre[:, cols], scalar=mean_var[:, 0:1], in1=gain(cols),
                 op0=ALU.subtract, op1=ALU.mult,
             )
-        if 1 <= step <= N_TILES:
-            cols = tile_cols(step - 1)
+        if 1 <= step <= len(pieces):
+            cols = pieces[step - 1]
             nc.vector.scalar_tensor_tensor(
-                out=gate[:, cols], in0=gate[:, cols], scalar=rstd[:], in1=shift[step - 1],
+                out=gate[:, cols], in0=gate[:, cols], scalar=rstd[:], in1=shift(cols),
                 op0=ALU.mult, op1=ALU.add,
             )
             nc.scalar.activation(out=gate[:, cols], in_=gate[:, cols], func=ACT.Sigmoid)
         if step >= 2:
-            finish(step - 2)
+            finish(pieces[step - 2])
 
 
 def tile_layernormlstmcell_pb_kernel(
@@ -244,25 +257,22 @@ def tile_layernormlstmcell_pb_kernel(
         acc_f = open_round(psum, FORGET_TILES)
         accumulate(nc, acc_f, (x_codes, x_scales, words[0], 0), planes, first=True, last=False)
         bias_f = spread_row_in_sbuf(nc, psum, keep, rows, 0, ident_bf)
-        gain_f = spread_row_in_sbuf(nc, psum, keep, rows, 1, ident_bf)
-        shift_f = spread_row_in_sbuf(nc, psum, keep, rows, 2, ident_bf)
         bias_o = spread_row_in_sbuf(nc, psum, keep, rows, 3, ident_bf)
+        gain_f = spread_row_in_psum(nc, psum, rows, 1, ident_bf)
+        shift_f = spread_row_in_psum(nc, psum, rows, 2, ident_bf)
         accumulate(nc, acc_f, (h_codes, h_scales, words[1], 1), planes, first=False, last=True)
         close_round(nc, acc_f, bias_f, pre_f, stats_f)
         cell = work.tile([P, N], F32)
         tanh_c = work.tile([P, N], F32)
 
-        def update_cell(j):
-            cols = tile_cols(j)
-            nc.vector.tensor_tensor(out=cell[:, cols], in0=cell[:, cols], in1=c_old[:, cols], op=ALU.mult)
-            nc.vector.tensor_tensor(out=cell[:, cols], in0=cell[:, cols], in1=ic_sb[:, cols], op=ALU.add)
+        def update_cell(cols):
+            nc.gpsimd.tensor_tensor(out=cell[:, cols], in0=cell[:, cols], in1=c_old[:, cols], op=ALU.mult)
+            nc.gpsimd.tensor_tensor(out=cell[:, cols], in0=cell[:, cols], in1=ic_sb[:, cols], op=ALU.add)
             nc.scalar.activation(out=tanh_c[:, cols], in_=cell[:, cols], func=ACT.Tanh)
 
-        layer_norm_sigmoid(nc, small, pre_f, stats_f, gain_f, shift_f, neg_half, cell, update_cell)
+        layer_norm_sigmoid(nc, small, pre_f, stats_f, gain_f, shift_f, neg_half, cell, column_pieces(FORGET_WIDTHS), update_cell)
         nc.sync.dma_start(out=c_new, in_=cell[:])
 
-        gain_o = spread_row_in_psum(nc, psum, rows, 4, ident_bf)
-        shift_o = spread_row_in_psum(nc, psum, rows, 5, ident_bf)
         pre_o = work.tile([P, N], F32, tag="pre")
         stats_o = small.tile([P, N_TILES, 6], F32)
         for tiles in OUTPUT_ROUNDS:
@@ -270,12 +280,14 @@ def tile_layernormlstmcell_pb_kernel(
             accumulate(nc, acc_o, (x_codes, x_scales, words[2], 2), planes, first=True, last=False)
             accumulate(nc, acc_o, (h_codes, h_scales, words[3], 3), planes, first=False, last=True)
             close_round(nc, acc_o, bias_o, pre_o, stats_o)
+            if tiles == OUTPUT_ROUNDS[0]:
+                gain_o = spread_row_in_psum(nc, psum, rows, 4, ident_bf)
+                shift_o = spread_row_in_psum(nc, psum, rows, 5, ident_bf)
         hidden = work.tile([P, N], F32)
 
-        def update_hidden(j):
-            cols = tile_cols(j)
-            engine = nc.gpsimd if j < N_TILES // 2 else nc.vector
+        def update_hidden(cols):
+            engine = nc.gpsimd if cols.start == 0 else nc.vector
             engine.tensor_tensor(out=hidden[:, cols], in0=hidden[:, cols], in1=tanh_c[:, cols], op=ALU.mult)
             nc.sync.dma_start(out=h_new[:, cols], in_=hidden[:, cols])
 
-        layer_norm_sigmoid(nc, small, pre_o, stats_o, gain_o, shift_o, neg_half, hidden, update_hidden)
+        layer_norm_sigmoid(nc, small, pre_o, stats_o, gain_o, shift_o, neg_half, hidden, column_pieces(OUTPUT_WIDTHS), update_hidden)

@@ -27,8 +27,10 @@ FLOPS = 4 * 2 * P * K * N
 
 FORGET_TILES = (0, 1, 2, 3)
 
-FORGET_WIDTHS = (512, 512, 512, 512)
-OUTPUT_WIDTHS = (512, 512, 512, 256, 256)
+FOLD_COLS = 768
+
+ROW_F_BIAS, ROW_F_GAIN, ROW_F_SHIFT, ROW_O_BIAS, ROW_O_GAIN = range(5)
+ROW_O_SHIFT = 16
 OUTPUT_ROUNDS = ((0, 1, 2), (3,))
 
 
@@ -36,13 +38,9 @@ def tile_cols(j):
     return slice(j * N_TILE, (j + 1) * N_TILE)
 
 
-def column_pieces(widths):
-    pieces = []
-    start = 0
-    for width in widths:
-        pieces.append(slice(start, start + width))
-        start += width
-    return pieces
+def halves(cols):
+    middle = (cols.start + cols.stop) // 2
+    return slice(cols.start, middle), slice(middle, cols.stop)
 
 
 def load_scale_planes(nc, planes, w, scales):
@@ -88,25 +86,27 @@ def quantise_activation(nc, pool, psum, raw, ident, codes, scales, name):
     )
 
 
-def spread_row(nc, psum, rows, r, ident_bf):
+def spread_row(nc, psum, rows, r, ident_bf, first=0):
     pick_row = ident_bf[:, r : r + 1].to_broadcast([P, P])
     banks = []
     for half in range(2):
         bank = psum.tile([P, 2 * N_TILE], BF16, tag="bank")
         for i in range(2):
-            nc.tensor.matmul(
-                out=bank[:, tile_cols(i)],
-                lhsT=pick_row,
-                rhs=rows[:, tile_cols(2 * half + i)],
-                start=True,
-                stop=True,
-            )
+            skip = min(max(first - (2 * half + i) * N_TILE, 0), N_TILE)
+            if skip < N_TILE:
+                nc.tensor.matmul(
+                    out=bank[:, i * N_TILE + skip : (i + 1) * N_TILE],
+                    lhsT=pick_row,
+                    rhs=rows[:, (2 * half + i) * N_TILE + skip : (2 * half + i + 1) * N_TILE],
+                    start=True,
+                    stop=True,
+                )
         banks.append(bank)
     return banks
 
 
-def spread_row_in_psum(nc, psum, rows, r, ident_bf):
-    banks = spread_row(nc, psum, rows, r, ident_bf)
+def spread_row_in_psum(nc, psum, rows, r, ident_bf, first=0):
+    banks = spread_row(nc, psum, rows, r, ident_bf, first)
     width = 2 * N_TILE
     return lambda cols: banks[cols.start // width][:, cols.start % width : (cols.stop - 1) % width + 1]
 
@@ -150,27 +150,33 @@ def close_round(nc, acc, bias, pre, stats):
             nc.vector.tensor_scalar_add(out=stats[:, j, 2:3], in0=stats[:, j, 2:3], scalar1=N * EPS)
 
 
-def layer_norm_sigmoid(nc, small, pre, stats, gain, shift, neg_half, gate, pieces, finish):
+def close_last_tile(nc, acc, bias, pre, stats):
+    last = N_TILES - 1
+    parts = halves(tile_cols(last))
+    for i, cols in enumerate(parts):
+        bank = acc[last][:, i * N_TILE // 2 : (i + 1) * N_TILE // 2]
+        nc.vector.tensor_tensor(out=pre[:, cols], in0=bank, in1=bias(cols), op=ALU.add)
+    for i, cols in enumerate(parts):
+        nc.vector.bn_stats(out=stats[:, last + i, :], in_=pre[:, cols])
+
+
+def aggregate(nc, small, stats):
     mean_var = small.tile([P, 2], F32)
     nc.vector.bn_aggr(out=mean_var[:], in_=stats[:].rearrange("p j s -> p (j s)"))
-    rstd = small.tile([P, 1], F32)
-    nc.gpsimd.tensor_tensor(out=rstd[:], in0=mean_var[:, 1:2], in1=neg_half[:], op=ALU.pow)
-    for step in range(len(pieces) + 2):
-        if step < len(pieces):
-            cols = pieces[step]
-            nc.vector.scalar_tensor_tensor(
-                out=gate[:, cols], in0=pre[:, cols], scalar=mean_var[:, 0:1], in1=gain(cols),
-                op0=ALU.subtract, op1=ALU.mult,
-            )
-        if 1 <= step <= len(pieces):
-            cols = pieces[step - 1]
-            nc.vector.scalar_tensor_tensor(
-                out=gate[:, cols], in0=gate[:, cols], scalar=rstd[:], in1=shift(cols),
-                op0=ALU.mult, op1=ALU.add,
-            )
-            nc.scalar.activation(out=gate[:, cols], in_=gate[:, cols], func=ACT.Sigmoid)
-        if step >= 2:
-            finish(pieces[step - 2])
+    return mean_var[:, 0:1], mean_var[:, 1:2]
+
+
+def centre(nc, pre, mean, gain, gate, cols):
+    nc.vector.scalar_tensor_tensor(
+        out=gate[:, cols], in0=pre[:, cols], scalar=mean, in1=gain(cols), op0=ALU.subtract, op1=ALU.mult
+    )
+
+
+def squash(nc, rstd, shift, gate, cols):
+    nc.vector.scalar_tensor_tensor(
+        out=gate[:, cols], in0=gate[:, cols], scalar=rstd, in1=shift(cols), op0=ALU.mult, op1=ALU.add
+    )
+    nc.scalar.activation(out=gate[:, cols], in_=gate[:, cols], func=ACT.Sigmoid)
 
 
 def tile_layernormlstmcell_pb_kernel(
@@ -213,20 +219,27 @@ def tile_layernormlstmcell_pb_kernel(
         h_scales = keep.tile([P, GROUPS * P], U8, align_bytes=64)
         c_old = keep.tile([P, N], BF16)
         ic_sb = keep.tile([P, N], BF16)
-        neg_half = keep.tile([P, 1], F32)
+        powers = keep.tile([P, 2], F32)
+        row_stats = keep.tile([P, P], F32)
+        ident = keep.tile([P, P], F32)
+        fold_rows = keep.tile([P, FOLD_COLS], F32)
         rows = keep.tile([P, N], BF16)
         ident_bf = keep.tile([P, P], BF16)
-        vectors = (Wf_b, lnf_g, lnf_b, Wo_b, lno_g, lno_b)
+        vectors = (
+            (ROW_F_BIAS, Wf_b), (ROW_F_GAIN, lnf_g), (ROW_F_SHIFT, lnf_b),
+            (ROW_O_BIAS, Wo_b), (ROW_O_GAIN, lno_g), (ROW_O_SHIFT, lno_b),
+        )
 
         with tc.tile_pool(name="head", bufs=1) as head:
-            ident = head.tile([P, P], F32)
             make_identity(nc, ident[:])
             for w in range(2):
                 nc.vector.memset(planes[:, w, :].bitcast(I32), 0)
             nc.vector.memset(rows[:].bitcast(I32), 0)
             for w in range(2, 4):
                 nc.vector.memset(planes[:, w, :].bitcast(I32), 0)
-            nc.vector.memset(neg_half[:], -0.5)
+            nc.vector.memset(powers[:, 0:1], 0.5)
+            nc.vector.memset(powers[:, 1:2], -0.5)
+            nc.vector.memset(row_stats[:], 0.0)
             nc.vector.tensor_copy(out=ident_bf[:], in_=ident[:])
 
             x_raw = head.tile([P, K], BF16)
@@ -234,7 +247,7 @@ def tile_layernormlstmcell_pb_kernel(
             h_raw = head.tile([P, K], BF16)
             nc.sync.dma_start(out=h_raw[:], in_=h)
             load_scale_planes(nc, planes, 0, Wf_w_scales)
-            for r, vector in enumerate(vectors):
+            for r, vector in vectors:
                 nc.gpsimd.dma_start(out=rows[r : r + 1, :], in_=vector.unsqueeze(0))
             load_scale_planes(nc, planes, 1, Uf_w_scales)
             load_scale_planes(nc, planes, 2, Wo_w_scales)
@@ -256,38 +269,81 @@ def tile_layernormlstmcell_pb_kernel(
         stats_f = small.tile([P, N_TILES, 6], F32)
         acc_f = open_round(psum, FORGET_TILES)
         accumulate(nc, acc_f, (x_codes, x_scales, words[0], 0), planes, first=True, last=False)
-        bias_f = spread_row_in_sbuf(nc, psum, keep, rows, 0, ident_bf)
-        bias_o = spread_row_in_sbuf(nc, psum, keep, rows, 3, ident_bf)
-        gain_f = spread_row_in_psum(nc, psum, rows, 1, ident_bf)
-        shift_f = spread_row_in_psum(nc, psum, rows, 2, ident_bf)
+        bias_f = spread_row_in_sbuf(nc, psum, keep, rows, ROW_F_BIAS, ident_bf)
+        bias_o = spread_row_in_sbuf(nc, psum, keep, rows, ROW_O_BIAS, ident_bf)
+        gain_f = spread_row_in_psum(nc, psum, rows, ROW_F_GAIN, ident_bf)
+        shift_f = spread_row_in_psum(nc, psum, rows, ROW_F_SHIFT, ident_bf)
+        nc.scalar.copy(out=fold_rows[:], in_=rows[:, :FOLD_COLS])
         accumulate(nc, acc_f, (h_codes, h_scales, words[1], 1), planes, first=False, last=True)
         close_round(nc, acc_f, bias_f, pre_f, stats_f)
         cell = work.tile([P, N], F32)
         tanh_c = work.tile([P, N], F32)
 
-        def update_cell(cols):
-            nc.gpsimd.tensor_tensor(out=cell[:, cols], in0=cell[:, cols], in1=c_old[:, cols], op=ALU.mult)
-            nc.gpsimd.tensor_tensor(out=cell[:, cols], in0=cell[:, cols], in1=ic_sb[:, cols], op=ALU.add)
-            nc.scalar.activation(out=tanh_c[:, cols], in_=cell[:, cols], func=ACT.Tanh)
-
-        layer_norm_sigmoid(nc, small, pre_f, stats_f, gain_f, shift_f, neg_half, cell, column_pieces(FORGET_WIDTHS), update_cell)
+        mean_f, var_f = aggregate(nc, small, stats_f)
+        rstd_f = small.tile([P, 1], F32)
+        nc.gpsimd.tensor_tensor(out=rstd_f[:], in0=var_f, in1=powers[:, 1:2], op=ALU.pow)
+        for step in range(N_TILES + 2):
+            if step < N_TILES:
+                centre(nc, pre_f, mean_f, gain_f, cell, tile_cols(step))
+            if 1 <= step <= N_TILES:
+                squash(nc, rstd_f[:], shift_f, cell, tile_cols(step - 1))
+            if step >= 2:
+                cols = tile_cols(step - 2)
+                nc.gpsimd.tensor_tensor(out=cell[:, cols], in0=cell[:, cols], in1=c_old[:, cols], op=ALU.mult)
+                nc.gpsimd.tensor_tensor(out=cell[:, cols], in0=cell[:, cols], in1=ic_sb[:, cols], op=ALU.add)
+                nc.scalar.activation(out=tanh_c[:, cols], in_=cell[:, cols], func=ACT.Tanh)
         nc.sync.dma_start(out=c_new, in_=cell[:])
 
         pre_o = work.tile([P, N], F32, tag="pre")
-        stats_o = small.tile([P, N_TILES, 6], F32)
-        for tiles in OUTPUT_ROUNDS:
-            acc_o = open_round(psum, tiles)
+        stats_o = small.tile([P, N_TILES + 1, 6], F32)
+        hidden = work.tile([P, N], F32)
+        acc_o = open_round(psum, OUTPUT_ROUNDS[0])
+        accumulate(nc, acc_o, (x_codes, x_scales, words[2], 2), planes, first=True, last=False)
+        accumulate(nc, acc_o, (h_codes, h_scales, words[3], 3), planes, first=False, last=True)
+        close_round(nc, acc_o, bias_o, pre_o, stats_o)
+        gain_o = spread_row_in_psum(nc, psum, rows, ROW_O_GAIN, ident_bf)
+        shift_o = spread_row_in_psum(nc, psum, rows, ROW_O_SHIFT, ident_bf, first=FOLD_COLS)
+
+        folds = (slice(0, N_TILE), slice(N_TILE, FOLD_COLS))
+        with tc.manual_schedule():
+            for cols in folds:
+                nc.vector.tensor_tensor(out=hidden[:, cols], in0=pre_o[:, cols], in1=gain_o(cols), op=ALU.mult)
+            acc_o = open_round(psum, OUTPUT_ROUNDS[1])
             accumulate(nc, acc_o, (x_codes, x_scales, words[2], 2), planes, first=True, last=False)
             accumulate(nc, acc_o, (h_codes, h_scales, words[3], 3), planes, first=False, last=True)
-            close_round(nc, acc_o, bias_o, pre_o, stats_o)
-            if tiles == OUTPUT_ROUNDS[0]:
-                gain_o = spread_row_in_psum(nc, psum, rows, 4, ident_bf)
-                shift_o = spread_row_in_psum(nc, psum, rows, 5, ident_bf)
-        hidden = work.tile([P, N], F32)
+            close_last_tile(nc, acc_o, bias_o, pre_o, stats_o)
+            folded = []
+            for i, cols in enumerate(folds):
+                bank = psum.tile([P, N_TILE], F32, tag="bank", name="folded%d" % i)
+                folded.append(bank[:, : cols.stop - cols.start])
+                nc.tensor.matmul(out=folded[i], lhsT=ident[:], rhs=hidden[:, cols], start=True, stop=False)
 
-        def update_hidden(cols):
-            engine = nc.gpsimd if cols.start == 0 else nc.vector
-            engine.tensor_tensor(out=hidden[:, cols], in0=hidden[:, cols], in1=tanh_c[:, cols], op=ALU.mult)
-            nc.sync.dma_start(out=h_new[:, cols], in_=hidden[:, cols])
+            mean_o, var_o = aggregate(nc, small, stats_o)
+            nc.vector.tensor_scalar_mul(out=row_stats[:, ROW_O_GAIN : ROW_O_GAIN + 1], in0=mean_o, scalar1=-1.0)
+            nc.gpsimd.tensor_tensor(
+                out=row_stats[:, ROW_O_SHIFT : ROW_O_SHIFT + 2], in0=var_o.to_broadcast([P, 2]), in1=powers[:], op=ALU.pow
+            )
+            rstd_o = row_stats[:, ROW_O_SHIFT + 1 : ROW_O_SHIFT + 2]
+            flipped = psum.tile([P, P], F32, tag="bank", name="flipped_stats")
+            nc.tensor.transpose(flipped[:], row_stats[:], ident[:])
+            stat_rows = small.tile([P, P], F32)
+            nc.scalar.copy(out=stat_rows[:], in_=flipped[:])
+            for i, cols in enumerate(folds):
+                nc.tensor.matmul(out=folded[i], lhsT=stat_rows[:], rhs=fold_rows[:, cols], start=False, stop=True)
 
-        layer_norm_sigmoid(nc, small, pre_o, stats_o, gain_o, shift_o, neg_half, hidden, column_pieces(OUTPUT_WIDTHS), update_hidden)
+            def fold_sigmoid(i):
+                nc.scalar.activation(out=hidden[:, folds[i]], in_=folded[i], func=ACT.Sigmoid, scale=rstd_o)
+
+            rest = slice(FOLD_COLS, 2 * N_TILE)
+            third, fourth = tile_cols(2), tile_cols(3)
+            centre(nc, pre_o, mean_o, gain_o, hidden, third)
+            centre(nc, pre_o, mean_o, gain_o, hidden, fourth)
+            squash(nc, rstd_o, shift_o, hidden, third)
+            centre(nc, pre_o, mean_o, gain_o, hidden, rest)
+            squash(nc, rstd_o, shift_o, hidden, fourth)
+            fold_sigmoid(0)
+            squash(nc, rstd_o, shift_o, hidden, rest)
+            fold_sigmoid(1)
+            for cols in (third, fourth, folds[0], rest, folds[1]):
+                nc.vector.tensor_tensor(out=hidden[:, cols], in0=hidden[:, cols], in1=tanh_c[:, cols], op=ALU.mult)
+                nc.sync.dma_start(out=h_new[:, cols], in_=hidden[:, cols])

from contextlib import ExitStack

import concourse.mybir as mybir
from concourse.masks import make_identity

F32 = mybir.dt.float32
BF16 = mybir.dt.bfloat16
I32 = mybir.dt.int32
U32 = mybir.dt.uint32
U8 = mybir.dt.uint8
FP8X4 = mybir.dt.float8_e4m3fn_x4
ALU = mybir.AluOpType
ACT = mybir.ActivationFunctionType
AXIS = mybir.AxisListType

P = 128
PACK = 4
K_PASS = P * PACK
K = 2048
GROUPS = K // K_PASS
N = 2048
N_TILE = 512
N_TILES = N // N_TILE
EPS = 1e-5

FLOPS = 4 * 2 * P * K * N

FORGET_TILES = (0, 1, 2, 3)

FOLD_COLS = 768

ROW_F_BIAS, ROW_F_GAIN, ROW_F_SHIFT, ROW_O_BIAS, ROW_O_GAIN = range(5)
ROW_O_SHIFT = 16
OUTPUT_ROUNDS = ((0, 1, 2), (3,))


def tile_cols(j):
    return slice(j * N_TILE, (j + 1) * N_TILE)


def halves(cols):
    middle = (cols.start + cols.stop) // 2
    return slice(cols.start, middle), slice(middle, cols.stop)


def load_scale_planes(nc, planes, w, scales):
    for quadrant in range(4):
        nc.gpsimd.dma_start(
            out=planes[32 * quadrant : 32 * quadrant + 16, w, :].bitcast(F32),
            in_=scales[:, 4 * quadrant : 4 * quadrant + 4, :].bitcast(F32),
        )


def load_weight_round(nc, words, dram_words, tiles):
    cols = slice(tiles[0] * N_TILE, (tiles[-1] + 1) * N_TILE)
    for g in range(GROUPS):
        nc.sync.dma_start(
            out=words[:, g, cols].bitcast(I32),
            in_=dram_words[g, :, cols, :].rearrange("p n t -> p (n t)").bitcast(I32),
        )


def quantise_activation(nc, pool, psum, raw, ident, codes, scales, name):
    raw_words = raw[:].bitcast(F32)
    grouped = pool.tile([P, GROUPS, P, PACK], BF16, align_bytes=64, name=name)
    grouped_words = grouped[:].bitcast(F32)
    words_per_group = K_PASS // 2
    for pair in range(GROUPS // 2):
        flipped = psum.tile([P, 2, 2, P], F32, tag="bank")
        for i in range(2):
            g = 2 * pair + i
            for u in range(2):
                nc.tensor.transpose(
                    flipped[:, i, u, :],
                    raw_words[:, g * words_per_group + u : (g + 1) * words_per_group : 2],
                    ident[:],
                )
        nc.vector.tensor_copy(
            out=grouped_words[:, 2 * pair : 2 * pair + 2, :, :],
            in_=flipped[:].rearrange("p g u m -> p g m u"),
        )
    nc.vector.quantize_mx(
        out=codes[:].bitcast(FP8X4),
        scales=scales[:],
        in_=grouped[:].rearrange("p g m t -> p (g m t)"),
    )


def spread_row(nc, psum, rows, r, ident_bf, first=0):
    pick_row = ident_bf[:, r : r + 1].to_broadcast([P, P])
    banks = []
    for half in range(2):
        bank = psum.tile([P, 2 * N_TILE], BF16, tag="bank")
        for i in range(2):
            skip = min(max(first - (2 * half + i) * N_TILE, 0), N_TILE)
            if skip < N_TILE:
                nc.tensor.matmul(
                    out=bank[:, i * N_TILE + skip : (i + 1) * N_TILE],
                    lhsT=pick_row,
                    rhs=rows[:, (2 * half + i) * N_TILE + skip : (2 * half + i + 1) * N_TILE],
                    start=True,
                    stop=True,
                )
        banks.append(bank)
    return banks


def spread_row_in_psum(nc, psum, rows, r, ident_bf, first=0):
    banks = spread_row(nc, psum, rows, r, ident_bf, first)
    width = 2 * N_TILE
    return lambda cols: banks[cols.start // width][:, cols.start % width : (cols.stop - 1) % width + 1]


def spread_row_in_sbuf(nc, psum, keep, rows, r, ident_bf):
    banks = spread_row(nc, psum, rows, r, ident_bf)
    spread = keep.tile([P, N], BF16, name="spread%d" % r)
    for half in range(2):
        nc.scalar.copy(out=spread[:, half * 2 * N_TILE : (half + 1) * 2 * N_TILE], in_=banks[half][:])
    return lambda cols: spread[:, cols]


def open_round(psum, tiles):
    acc = {}
    for j in tiles:
        acc[j] = psum.tile([P, N_TILE], F32, tag="bank", name="acc%d" % j)
    return acc


def accumulate(nc, acc, operand, planes, first, last):
    codes, scales, words, w = operand
    for g in range(GROUPS):
        batch_cols = slice(g * P, (g + 1) * P)
        for j in acc:
            nc.tensor.matmul_mx(
                out=acc[j][:],
                lhsT=codes[:, batch_cols].bitcast(FP8X4),
                lhsT_scale=scales[:, batch_cols],
                rhs=words[:, g, tile_cols(j)].bitcast(FP8X4),
                rhs_scale=planes[PACK * g : P, w, tile_cols(j)],
                start=(first and g == 0),
                stop=(last and g == GROUPS - 1),
            )


def close_round(nc, acc, bias, pre, stats):
    for j in acc:
        nc.vector.tensor_tensor(out=pre[:, tile_cols(j)], in0=acc[j][:], in1=bias(tile_cols(j)), op=ALU.add)
        nc.vector.bn_stats(out=stats[:, j, :], in_=pre[:, tile_cols(j)])
        if j == 0:
            nc.vector.tensor_scalar_add(out=stats[:, j, 2:3], in0=stats[:, j, 2:3], scalar1=N * EPS)


def close_last_tile(nc, acc, bias, pre, stats):
    last = N_TILES - 1
    parts = halves(tile_cols(last))
    for i, cols in enumerate(parts):
        bank = acc[last][:, i * N_TILE // 2 : (i + 1) * N_TILE // 2]
        nc.vector.tensor_tensor(out=pre[:, cols], in0=bank, in1=bias(cols), op=ALU.add)
    for i, cols in enumerate(parts):
        nc.vector.bn_stats(out=stats[:, last + i, :], in_=pre[:, cols])


def aggregate(nc, small, stats):
    mean_var = small.tile([P, 2], F32)
    nc.vector.bn_aggr(out=mean_var[:], in_=stats[:].rearrange("p j s -> p (j s)"))
    return mean_var[:, 0:1], mean_var[:, 1:2]


def centre(nc, pre, mean, gain, gate, cols):
    nc.vector.scalar_tensor_tensor(
        out=gate[:, cols], in0=pre[:, cols], scalar=mean, in1=gain(cols), op0=ALU.subtract, op1=ALU.mult
    )


def squash(nc, rstd, shift, gate, cols):
    nc.vector.scalar_tensor_tensor(
        out=gate[:, cols], in0=gate[:, cols], scalar=rstd, in1=shift(cols), op0=ALU.mult, op1=ALU.add
    )
    nc.scalar.activation(out=gate[:, cols], in_=gate[:, cols], func=ACT.Sigmoid)


def tile_layernormlstmcell_pb_kernel(
    tc,
    x,
    h,
    c,
    ic_tilde,
    Wf_w_words,
    Wf_w_scales,
    Wf_b,
    Uf_w_words,
    Uf_w_scales,
    lnf_g,
    lnf_b,
    Wo_w_words,
    Wo_w_scales,
    Wo_b,
    Uo_w_words,
    Uo_w_scales,
    lno_g,
    lno_b,
    out_0,
    out_1,
):
    nc = tc.nc
    h_new, c_new = out_0, out_1
    with ExitStack() as stack:
        keep = stack.enter_context(tc.tile_pool(name="keep", bufs=1))
        small = stack.enter_context(tc.tile_pool(name="small", bufs=2))
        psum = stack.enter_context(tc.psum_pool(name="psum", bufs=8))

        planes = keep.tile([P, 4, N], U8, align_bytes=64)
        words = []
        for w in range(4):
            words.append(keep.tile([P, GROUPS, N], U32, align_bytes=64, name="words%d" % w))
        x_codes = keep.tile([P, GROUPS * P], U32, align_bytes=64)
        x_scales = keep.tile([P, GROUPS * P], U8, align_bytes=64)
        h_codes = keep.tile([P, GROUPS * P], U32, align_bytes=64)
        h_scales = keep.tile([P, GROUPS * P], U8, align_bytes=64)
        c_old = keep.tile([P, N], BF16)
        ic_sb = keep.tile([P, N], BF16)
        powers = keep.tile([P, 2], F32)
        row_stats = keep.tile([P, P], F32)
        ident = keep.tile([P, P], F32)
        fold_rows = keep.tile([P, FOLD_COLS], F32)
        rows = keep.tile([P, N], BF16)
        ident_bf = keep.tile([P, P], BF16)
        vectors = (
            (ROW_F_BIAS, Wf_b), (ROW_F_GAIN, lnf_g), (ROW_F_SHIFT, lnf_b),
            (ROW_O_BIAS, Wo_b), (ROW_O_GAIN, lno_g), (ROW_O_SHIFT, lno_b),
        )

        with tc.tile_pool(name="head", bufs=1) as head:
            make_identity(nc, ident[:])
            for w in range(2):
                nc.vector.memset(planes[:, w, :].bitcast(I32), 0)
            nc.vector.memset(rows[:].bitcast(I32), 0)
            for w in range(2, 4):
                nc.vector.memset(planes[:, w, :].bitcast(I32), 0)
            nc.vector.memset(powers[:, 0:1], 0.5)
            nc.vector.memset(powers[:, 1:2], -0.5)
            nc.vector.memset(row_stats[:], 0.0)
            nc.vector.tensor_copy(out=ident_bf[:], in_=ident[:])

            x_raw = head.tile([P, K], BF16)
            nc.sync.dma_start(out=x_raw[:], in_=x)
            h_raw = head.tile([P, K], BF16)
            nc.sync.dma_start(out=h_raw[:], in_=h)
            load_scale_planes(nc, planes, 0, Wf_w_scales)
            for r, vector in vectors:
                nc.gpsimd.dma_start(out=rows[r : r + 1, :], in_=vector.unsqueeze(0))
            load_scale_planes(nc, planes, 1, Uf_w_scales)
            load_scale_planes(nc, planes, 2, Wo_w_scales)
            load_scale_planes(nc, planes, 3, Uo_w_scales)
            load_weight_round(nc, words[0], Wf_w_words, FORGET_TILES)
            load_weight_round(nc, words[1], Uf_w_words, FORGET_TILES)
            nc.sync.dma_start(out=c_old[:], in_=c)
            nc.sync.dma_start(out=ic_sb[:], in_=ic_tilde)
            for tiles in OUTPUT_ROUNDS:
                load_weight_round(nc, words[2], Wo_w_words, tiles)
                load_weight_round(nc, words[3], Uo_w_words, tiles)

            quantise_activation(nc, head, psum, x_raw, ident, x_codes, x_scales, "x_grouped")
            quantise_activation(nc, head, psum, h_raw, ident, h_codes, h_scales, "h_grouped")

        work = stack.enter_context(tc.tile_pool(name="work", bufs=1))

        pre_f = work.tile([P, N], F32, tag="pre")
        stats_f = small.tile([P, N_TILES, 6], F32)
        acc_f = open_round(psum, FORGET_TILES)
        accumulate(nc, acc_f, (x_codes, x_scales, words[0], 0), planes, first=True, last=False)
        bias_f = spread_row_in_sbuf(nc, psum, keep, rows, ROW_F_BIAS, ident_bf)
        bias_o = spread_row_in_sbuf(nc, psum, keep, rows, ROW_O_BIAS, ident_bf)
        gain_f = spread_row_in_psum(nc, psum, rows, ROW_F_GAIN, ident_bf)
        shift_f = spread_row_in_psum(nc, psum, rows, ROW_F_SHIFT, ident_bf)
        nc.scalar.copy(out=fold_rows[:], in_=rows[:, :FOLD_COLS])
        accumulate(nc, acc_f, (h_codes, h_scales, words[1], 1), planes, first=False, last=True)
        close_round(nc, acc_f, bias_f, pre_f, stats_f)
        cell = work.tile([P, N], F32)
        tanh_c = work.tile([P, N], F32)

        mean_f, var_f = aggregate(nc, small, stats_f)
        rstd_f = small.tile([P, 1], F32)
        nc.gpsimd.tensor_tensor(out=rstd_f[:], in0=var_f, in1=powers[:, 1:2], op=ALU.pow)
        for step in range(N_TILES + 2):
            if step < N_TILES:
                centre(nc, pre_f, mean_f, gain_f, cell, tile_cols(step))
            if 1 <= step <= N_TILES:
                squash(nc, rstd_f[:], shift_f, cell, tile_cols(step - 1))
            if step >= 2:
                cols = tile_cols(step - 2)
                nc.gpsimd.tensor_tensor(out=cell[:, cols], in0=cell[:, cols], in1=c_old[:, cols], op=ALU.mult)
                nc.gpsimd.tensor_tensor(out=cell[:, cols], in0=cell[:, cols], in1=ic_sb[:, cols], op=ALU.add)
                nc.scalar.activation(out=tanh_c[:, cols], in_=cell[:, cols], func=ACT.Tanh)
        nc.sync.dma_start(out=c_new, in_=cell[:])

        pre_o = work.tile([P, N], F32, tag="pre")
        stats_o = small.tile([P, N_TILES + 1, 6], F32)
        hidden = work.tile([P, N], F32)
        acc_o = open_round(psum, OUTPUT_ROUNDS[0])
        accumulate(nc, acc_o, (x_codes, x_scales, words[2], 2), planes, first=True, last=False)
        accumulate(nc, acc_o, (h_codes, h_scales, words[3], 3), planes, first=False, last=True)
        close_round(nc, acc_o, bias_o, pre_o, stats_o)
        gain_o = spread_row_in_psum(nc, psum, rows, ROW_O_GAIN, ident_bf)
        shift_o = spread_row_in_psum(nc, psum, rows, ROW_O_SHIFT, ident_bf, first=FOLD_COLS)

        folds = (slice(0, N_TILE), slice(N_TILE, FOLD_COLS))
        with tc.manual_schedule():
            for cols in folds:
                nc.vector.tensor_tensor(out=hidden[:, cols], in0=pre_o[:, cols], in1=gain_o(cols), op=ALU.mult)
            acc_o = open_round(psum, OUTPUT_ROUNDS[1])
            accumulate(nc, acc_o, (x_codes, x_scales, words[2], 2), planes, first=True, last=False)
            accumulate(nc, acc_o, (h_codes, h_scales, words[3], 3), planes, first=False, last=True)
            close_last_tile(nc, acc_o, bias_o, pre_o, stats_o)
            folded = []
            for i, cols in enumerate(folds):
                bank = psum.tile([P, N_TILE], F32, tag="bank", name="folded%d" % i)
                folded.append(bank[:, : cols.stop - cols.start])
                nc.tensor.matmul(out=folded[i], lhsT=ident[:], rhs=hidden[:, cols], start=True, stop=False)

            mean_o, var_o = aggregate(nc, small, stats_o)
            nc.vector.tensor_scalar_mul(out=row_stats[:, ROW_O_GAIN : ROW_O_GAIN + 1], in0=mean_o, scalar1=-1.0)
            nc.gpsimd.tensor_tensor(
                out=row_stats[:, ROW_O_SHIFT : ROW_O_SHIFT + 2], in0=var_o.to_broadcast([P, 2]), in1=powers[:], op=ALU.pow
            )
            rstd_o = row_stats[:, ROW_O_SHIFT + 1 : ROW_O_SHIFT + 2]
            flipped = psum.tile([P, P], F32, tag="bank", name="flipped_stats")
            nc.tensor.transpose(flipped[:], row_stats[:], ident[:])
            stat_rows = small.tile([P, P], F32)
            nc.scalar.copy(out=stat_rows[:], in_=flipped[:])
            for i, cols in enumerate(folds):
                nc.tensor.matmul(out=folded[i], lhsT=stat_rows[:], rhs=fold_rows[:, cols], start=False, stop=True)

            def fold_sigmoid(i):
                nc.scalar.activation(out=hidden[:, folds[i]], in_=folded[i], func=ACT.Sigmoid, scale=rstd_o)

            rest = slice(FOLD_COLS, 2 * N_TILE)
            third, fourth = tile_cols(2), tile_cols(3)
            centre(nc, pre_o, mean_o, gain_o, hidden, third)
            centre(nc, pre_o, mean_o, gain_o, hidden, fourth)
            squash(nc, rstd_o, shift_o, hidden, third)
            centre(nc, pre_o, mean_o, gain_o, hidden, rest)
            squash(nc, rstd_o, shift_o, hidden, fourth)
            fold_sigmoid(0)
            squash(nc, rstd_o, shift_o, hidden, rest)
            fold_sigmoid(1)
            for cols in (third, fourth, folds[0], rest, folds[1]):
                nc.vector.tensor_tensor(out=hidden[:, cols], in0=hidden[:, cols], in1=tanh_c[:, cols], op=ALU.mult)
                nc.sync.dma_start(out=h_new[:, cols], in_=hidden[:, cols])
